import numpy as np
import ml_dtypes


BF16 = ml_dtypes.bfloat16


def bf(x):
    return np.asarray(x, np.float32).astype(BF16)


def f64(x):
    return np.asarray(x).astype(np.float64)


E2M1 = np.array([0.0, 0.5, 1.0, 1.5, 2.0, 3.0, 4.0, 6.0, -0.0, -0.5, -1.0, -1.5, -2.0, -3.0, -4.0, -6.0])


def pack_weight(w, fmt):
    k, n = w.shape
    w = f64(bf(w)).reshape(k // 32, 32, n)
    amax = np.abs(w).max(1)
    if fmt == "e4m3":
        byte = np.frexp(amax)[1] - 1 + 127 - 7
    else:
        mant, ex = np.frexp(amax / 6.0)
        byte = np.where(mant > 0.5, ex, ex - 1) + 127
    byte = np.clip(np.where(amax > 0, byte, 1), 1, 254)
    scaled = (w * np.exp2(127.0 - byte)[:, None, :]).reshape(k, n).astype(np.float32)
    by_word = np.ascontiguousarray(scaled.reshape(k // 512, 128, 4, n).transpose(0, 1, 3, 2))
    if fmt == "e4m3":
        words = by_word.astype(ml_dtypes.float8_e4m3fn).view(np.uint8)
    else:
        c = by_word.astype(ml_dtypes.float4_e2m1fn).view(np.uint8) & 0xF
        words = c[..., 0::2] | (c[..., 1::2] << 4)
    return np.ascontiguousarray(words), np.ascontiguousarray(byte.astype(np.uint8).reshape(k // 512, 16, n))


def unpack_weight(words, scales, fmt):
    g, p, n, _ = words.shape
    if fmt == "e4m3":
        vals = np.ascontiguousarray(words).view(ml_dtypes.float8_e4m3fn).astype(np.float64)
    else:
        nib = np.empty((g, p, n, 4), np.uint8)
        nib[..., 0::2] = words & 0xF
        nib[..., 1::2] = words >> 4
        vals = E2M1[nib]
    vals = vals * np.repeat(np.exp2(scales.astype(np.float64) - 127.0), 8, axis=1)[..., None]
    return vals.transpose(0, 1, 3, 2).reshape(g * 512, n)

def pack4(w):
    words, scales = pack_weight(w, "e2m1")
    return words.reshape(words.shape[0], 128, -1), scales


def unpack4(words, scales):
    return unpack_weight(words.reshape(words.shape[0], 128, -1, 2), scales, "e2m1")


def kspread(k):
    return np.exp2(np.repeat(np.random.randint(-6, 7, k // 32), 32).astype(np.float64))


B, N, D, H, DK, DV = 4, 1536, 4096, 8, 128, 128


def xnorm(x, g):
    n = np.sqrt(np.sum(x * x, axis=-1, keepdims=True))
    return x * g / n


def setup_inputs():
    s = kspread(D)
    queries = np.random.standard_normal((B, N, D)) * s
    queries_words, queries_scales = pack4(queries.reshape(B * N, D).T)
    Wq_words, Wq_scales = pack4(np.random.standard_normal((D, H * DK)) / np.sqrt(D) / s[:, None])
    return {
        "queries_words": queries_words,
        "queries_scales": queries_scales,
        "Wq_words": Wq_words,
        "Wq_scales": Wq_scales,
        "bq": bf(np.random.standard_normal(H * DK) * 0.1),
        "gamma": bf(np.random.standard_normal((1, H, 1, 1)) * 2.0),
    }


def reference(queries_words, queries_scales, Wq_words, Wq_scales, bq, gamma):
    q = ((unpack4(queries_words, queries_scales).T.reshape(B, N, D) @ unpack4(Wq_words, Wq_scales)) + f64(bq)).reshape(B, N, H, DK)
    return xnorm(q.transpose(0, 2, 1, 3), f64(gamma))

@@ -1,0 +1,181 @@
+from contextlib import ExitStack
+
+import concourse.mybir as mybir
+
+F32 = mybir.dt.float32
+BF16 = mybir.dt.bfloat16
+U8 = mybir.dt.uint8
+I32 = mybir.dt.int32
+FP4X4 = mybir.dt.float4_e2m1fn_x4
+ACT = mybir.ActivationFunctionType
+ALU = mybir.AluOpType
+
+B, NTOK, D, H, DK = 4, 1536, 4096, 8, 128
+T = B * NTOK
+C_OUT = H * DK
+FLOPS = 2 * T * D * C_OUT
+
+P = 128
+G = D // 512
+NB = 512
+HPU = NB // DK
+NHALF = C_OUT // NB
+NTILE = T // P
+NUNIT = NTILE * NHALF
+HEAD_UNITS = 8
+GROUPS = ((0, 2), (2, 8))
+CHUNKS = (512, 512, 1024, 1024, 1024, 1024, 1024)
+
+
+def tile_ufoattention_pb_kernel(tc, queries_words, queries_scales, Wq_words, Wq_scales, bq, gamma, out):
+    nc = tc.nc
+    with ExitStack() as ctx:
+        keep = ctx.enter_context(tc.tile_pool(name="keep", bufs=1))
+        ypool = ctx.enter_context(tc.tile_pool(name="ypool", bufs=8))
+        stat = ctx.enter_context(tc.tile_pool(name="stat", bufs=4))
+        psum = ctx.enter_context(tc.psum_pool(name="psum", bufs=8))
+        ctx.enter_context(tc.manual_schedule())
+
+        def load_scales(name, src, g0, g1, c0, c1):
+            plane = keep.tile([P, g1 - g0, c1 - c0], U8, name=name, align_bytes=64)
+            nc.vector.memset(plane[:].bitcast(I32), 0)
+            for q in range(4):
+                nc.sync.dma_start(
+                    out=plane[32 * q : 32 * q + 4, :, :].bitcast(I32),
+                    in_=src[g0:g1, 4 * q : 4 * q + 4, c0:c1].rearrange("g r n -> r g n").bitcast(I32),
+                )
+            return plane
+
+        def load_codes(name, src, g0, g1, c0, c1):
+            codes = keep.tile([P, g1 - g0, 2 * (c1 - c0)], U8, name=name, align_bytes=64)
+            nc.sync.dma_start(
+                out=codes[:].bitcast(I32),
+                in_=src[g0:g1, :, 2 * c0 : 2 * c1].rearrange("g p n -> p g n").bitcast(I32),
+            )
+            return codes
+
+        brow = keep.tile([P, 3 * NB], BF16, name="brow")
+        ones = keep.tile([P, P], BF16, name="ones")
+        warm = keep.tile([P, 1], F32, name="warm")
+        nc.gpsimd.memset(brow[:], 0.0)
+        nc.gpsimd.memset(ones[:], 1.0)
+        nc.gpsimd.memset(warm[:], 1.0)
+        nc.scalar.dma_start(out=brow[0:1, 0:C_OUT], in_=bq.rearrange("(o n) -> o n", o=1))
+        nc.scalar.dma_start(out=brow[0:1, C_OUT : C_OUT + H], in_=gamma.rearrange("a h b c -> a (h b c)"))
+        nc.scalar.activation(out=warm[:], in_=warm[:], func=ACT.Sqrt)
+
+        wc = {}
+        ws = {}
+        qc = {}
+        qs = {}
+        C0 = CHUNKS[0]
+        (a0, a1), (b0, b1) = GROUPS
+        wc[0] = load_codes("wc0", Wq_words, 0, 1, 0, C_OUT)
+        qcA = load_codes("qc0a", queries_words, a0, a1, 0, C0)
+        wsA = load_scales("wsa", Wq_scales, a0, a1, 0, C_OUT)
+        qsA = load_scales("qs0a", queries_scales, a0, a1, 0, C0)
+        wc[1] = load_codes("wc1", Wq_words, 1, 2, 0, C_OUT)
+        wsB = load_scales("wsb", Wq_scales, b0, b1, 0, C_OUT)
+        qsB = load_scales("qs0b", queries_scales, b0, b1, 0, C0)
+        wc[2] = load_codes("wc2", Wq_words, 2, 3, 0, C_OUT)
+        qcB = load_codes("qc0b", queries_words, b0, b1, 0, C0)
+        for g in range(3, G):
+            wc[g] = load_codes("wc%d" % g, Wq_words, g, g + 1, 0, C_OUT)
+        for g in range(G):
+            ws[g] = (wsA, g - a0) if g < a1 else (wsB, g - b0)
+        for j in range(C0 // P):
+            for g in range(G):
+                qc[(j, g)] = (qcA, g - a0, j) if g < a1 else (qcB, g - b0, j)
+                qs[(j, g)] = (qsA, g - a0, j) if g < a1 else (qsB, g - b0, j)
+        c0 = C0
+        for ci in range(1, len(CHUNKS)):
+            c1 = c0 + CHUNKS[ci]
+            s_t = load_scales("qs%d" % ci, queries_scales, 0, G, c0, c1)
+            c_t = load_codes("qc%d" % ci, queries_words, 0, G, c0, c1)
+            for jj in range(CHUNKS[ci] // P):
+                for g in range(G):
+                    qc[(c0 // P + jj, g)] = (c_t, g, jj)
+                    qs[(c0 // P + jj, g)] = (s_t, g, jj)
+            c0 = c1
+
+        bias = keep.tile([P, C_OUT], F32, name="bias")
+        gam = keep.tile([P, H], F32, name="gam")
+        for i in range(3):
+            bps = psum.tile([P, NB], F32, name="acc")
+            nc.tensor.matmul(out=bps[:], lhsT=ones[:], rhs=brow[:, NB * i : NB * (i + 1)], start=True, stop=True)
+            if i < 2:
+                nc.scalar.copy(out=bias[:, NB * i : NB * (i + 1)], in_=bps[:])
+            else:
+                nc.scalar.copy(out=gam[:], in_=bps[:, 0:H])
+
+        junk = keep.tile([P, DK], F32, name="junk")
+
+        def mm(acc, u, g):
+            j, half = u // NHALF, u % NHALF
+            ct, gi, jj = qc[(j, g)]
+            st, gs, js = qs[(j, g)]
+            wst, wg = ws[g]
+            nc.tensor.matmul_mx(
+                out=acc[:],
+                lhsT=ct[:, gi, 2 * P * jj : 2 * P * (jj + 1)].bitcast(FP4X4),
+                lhsT_scale=st[:, gs, P * js : P * (js + 1)],
+                rhs=wc[g][:, 0, 2 * NB * half : 2 * NB * (half + 1)].bitcast(FP4X4),
+                rhs_scale=wst[:, wg, NB * half : NB * (half + 1)],
+                start=(g == 0),
+                stop=(g == G - 1),
+            )
+
+        ys = {}
+        rs = {}
+
+        def add_and_square(acc, u):
+            half = u % NHALF
+            y = ypool.tile([P, NB], F32, name="y")
+            nc.vector.tensor_tensor(out=y[:], in0=acc[:], in1=bias[:, NB * half : NB * (half + 1)], op=ALU.add)
+            ss = stat.tile([P, HPU], F32, name="ss")
+            for h in range(HPU):
+                nc.scalar.activation(
+                    out=junk[:], in_=y[:, DK * h : DK * (h + 1)], func=ACT.Square, accum_out=ss[:, h : h + 1]
+                )
+            nrm = stat.tile([P, HPU], F32, name="nrm")
+            nc.scalar.activation(out=nrm[:], in_=ss[:], func=ACT.Sqrt)
+            ys[u] = y
+            rs[u] = nrm
+
+        def scale_and_store(u):
+            j, half = u // NHALF, u % NHALF
+            y = ys[u]
+            nrm = rs[u]
+            rinv = stat.tile([P, HPU], F32, name="rinv")
+            nc.vector.reciprocal(out=rinv[:], in_=nrm[:])
+            for h in range(HPU):
+                hh = HPU * half + h
+                nc.vector.tensor_scalar(
+                    out=y[:, DK * h : DK * (h + 1)],
+                    in0=y[:, DK * h : DK * (h + 1)],
+                    scalar1=rinv[:, h : h + 1],
+                    scalar2=gam[:, hh : hh + 1],
+                    op0=ALU.mult,
+                    op1=ALU.mult,
+                )
+            b, t0 = j // (NTOK // P), (j % (NTOK // P)) * P
+            nc.scalar.dma_start(
+                out=out[b, HPU * half : HPU * (half + 1), t0 : t0 + P, :].rearrange("h t d -> t h d"),
+                in_=y[:].rearrange("p (h d) -> p h d", h=HPU),
+            )
+
+        accs = {}
+        for u in range(HEAD_UNITS):
+            accs[u] = psum.tile([P, NB], F32, name="acc")
+        for g in range(G):
+            for u in range(HEAD_UNITS):
+                mm(accs[u], u, g)
+        for u in range(NUNIT):
+            if u >= HEAD_UNITS:
+                accs[u] = psum.tile([P, NB], F32, name="acc")
+                for g in range(G):
+                    mm(accs[u], u, g)
+            add_and_square(accs[u], u)
+            if u >= 1:
+                scale_and_store(u - 1)
+        scale_and_store(NUNIT - 1)

@@ -18,13 +18,17 @@ FLOPS = 2 * T * D * C_OUT
 P = 128
 G = D // 512
 NB = 512
-HPU = NB // DK
-NHALF = C_OUT // NB
 NTILE = T // P
-NUNIT = NTILE * NHALF
 HEAD_UNITS = 8
-GROUPS = ((0, 2), (2, 8))
-CHUNKS = (512, 512, 1024, 1024, 1024, 1024, 1024)
+CHUNK = 512
+NCHUNK = T // CHUNK
+UNITS_PER_CHUNK = (CHUNK // P) * (C_OUT // NB)
+GROUPS = ((0, 4), (4, 8))
+W_CODE_GROUPS = ((0, 1), (1, 2), (2, 3), (3, 4), (4, 6), (6, 8))
+LOAD_AHEAD = 2
+WARM_BEFORE_BIAS = 3
+WARM_AFTER_BIAS = 7
+TAIL_W = 256
 
 
 def tile_ufoattention_pb_kernel(tc, queries_words, queries_scales, Wq_words, Wq_scales, bq, gamma, out):
@@ -36,15 +40,17 @@ def tile_ufoattention_pb_kernel(tc, queries_words, queries_scales, Wq_words, Wq_
         psum = ctx.enter_context(tc.psum_pool(name="psum", bufs=8))
         ctx.enter_context(tc.manual_schedule())
 
-        def load_scales(name, src, g0, g1, c0, c1):
-            plane = keep.tile([P, g1 - g0, c1 - c0], U8, name=name, align_bytes=64)
+        def new_plane(name, g0, g1, width):
+            plane = keep.tile([P, g1 - g0, width], U8, name=name, align_bytes=64)
             nc.vector.memset(plane[:].bitcast(I32), 0)
+            return plane
+
+        def load_scales(plane, src, g0, g1, c0, c1):
             for q in range(4):
                 nc.sync.dma_start(
                     out=plane[32 * q : 32 * q + 4, :, :].bitcast(I32),
                     in_=src[g0:g1, 4 * q : 4 * q + 4, c0:c1].rearrange("g r n -> r g n").bitcast(I32),
                 )
-            return plane
 
         def load_codes(name, src, g0, g1, c0, c1):
             codes = keep.tile([P, g1 - g0, 2 * (c1 - c0)], U8, name=name, align_bytes=64)
@@ -54,73 +60,100 @@ def tile_ufoattention_pb_kernel(tc, queries_words, queries_scales, Wq_words, Wq_
             )
             return codes
 
-        brow = keep.tile([P, 3 * NB], BF16, name="brow")
-        ones = keep.tile([P, P], BF16, name="ones")
+        brow = keep.tile([P, C_OUT], BF16, name="brow")
+        ones = keep.tile([P, NB], BF16, name="ones")
         warm = keep.tile([P, 1], F32, name="warm")
-        nc.gpsimd.memset(brow[:], 0.0)
-        nc.gpsimd.memset(ones[:], 1.0)
+        gam_bf = keep.tile([P, H], BF16, name="gam_bf")
+        gam = keep.tile([P, H], F32, name="gam")
+        bias = keep.tile([P, C_OUT], F32, name="bias")
+        junk = keep.tile([P, DK], F32, name="junk")
         nc.gpsimd.memset(warm[:], 1.0)
-        nc.scalar.dma_start(out=brow[0:1, 0:C_OUT], in_=bq.rearrange("(o n) -> o n", o=1))
-        nc.scalar.dma_start(out=brow[0:1, C_OUT : C_OUT + H], in_=gamma.rearrange("a h b c -> a (h b c)"))
-        nc.scalar.activation(out=warm[:], in_=warm[:], func=ACT.Sqrt)
+        nc.gpsimd.memset(brow[:].bitcast(F32), 0.0)
+        nc.scalar.dma_start(out=brow[0:1, :], in_=bq.rearrange("(o n) -> o n", o=1))
+        nc.gpsimd.memset(ones[:], 1.0)
+        nc.gpsimd.dma_start(out=gam_bf[:], in_=gamma.rearrange("a h b c -> (a h b c)").partition_broadcast(P))
+        nc.scalar.activation(out=warm[:], in_=warm[:], func=ACT.Abs_reciprocal_sqrt)
+
+        (a0, a1), (b0, b1) = GROUPS
+        wsA = new_plane("wsa", a0, a1, C_OUT)
+        qsA = new_plane("qs0a", a0, a1, CHUNK)
+        wsB = new_plane("wsb", b0, b1, C_OUT)
+        qsB = new_plane("qs0b", b0, b1, CHUNK)
+        planes = {}
+        for c in range(1, NCHUNK):
+            planes[c] = new_plane("qs%d" % c, 0, G, CHUNK)
+        nc.vector.tensor_copy(out=gam[:], in_=gam_bf[:])
 
         wc = {}
         ws = {}
         qc = {}
         qs = {}
-        C0 = CHUNKS[0]
-        (a0, a1), (b0, b1) = GROUPS
-        wc[0] = load_codes("wc0", Wq_words, 0, 1, 0, C_OUT)
-        qcA = load_codes("qc0a", queries_words, a0, a1, 0, C0)
-        wsA = load_scales("wsa", Wq_scales, a0, a1, 0, C_OUT)
-        qsA = load_scales("qs0a", queries_scales, a0, a1, 0, C0)
-        wc[1] = load_codes("wc1", Wq_words, 1, 2, 0, C_OUT)
-        wsB = load_scales("wsb", Wq_scales, b0, b1, 0, C_OUT)
-        qsB = load_scales("qs0b", queries_scales, b0, b1, 0, C0)
-        wc[2] = load_codes("wc2", Wq_words, 2, 3, 0, C_OUT)
-        qcB = load_codes("qc0b", queries_words, b0, b1, 0, C0)
-        for g in range(3, G):
-            wc[g] = load_codes("wc%d" % g, Wq_words, g, g + 1, 0, C_OUT)
+
+        def load_w_codes(i):
+            g0, g1 = W_CODE_GROUPS[i]
+            t = load_codes("wc%d" % i, Wq_words, g0, g1, 0, C_OUT)
+            for g in range(g0, g1):
+                wc[g] = (t, g - g0)
+
+        load_w_codes(0)
+        qcA = load_codes("qc0a", queries_words, a0, a1, 0, CHUNK)
+        load_scales(wsA, Wq_scales, a0, a1, 0, C_OUT)
+        load_scales(qsA, queries_scales, a0, a1, 0, CHUNK)
+        load_w_codes(1)
+        load_w_codes(2)
+        load_w_codes(3)
+        load_scales(wsB, Wq_scales, b0, b1, 0, C_OUT)
+        load_scales(qsB, queries_scales, b0, b1, 0, CHUNK)
+        qcB = load_codes("qc0b", queries_words, b0, b1, 0, CHUNK)
+        load_w_codes(4)
+        load_w_codes(5)
         for g in range(G):
             ws[g] = (wsA, g - a0) if g < a1 else (wsB, g - b0)
-        for j in range(C0 // P):
+            qc[(0, g)] = (qcA, g - a0) if g < a1 else (qcB, g - b0)
+            qs[(0, g)] = (qsA, g - a0) if g < a1 else (qsB, g - b0)
+
+        def load_chunk(c):
+            load_scales(planes[c], queries_scales, 0, G, CHUNK * c, CHUNK * (c + 1))
+            t = load_codes("qc%d" % c, queries_words, 0, G, CHUNK * c, CHUNK * (c + 1))
             for g in range(G):
-                qc[(j, g)] = (qcA, g - a0, j) if g < a1 else (qcB, g - b0, j)
-                qs[(j, g)] = (qsA, g - a0, j) if g < a1 else (qsB, g - b0, j)
-        c0 = C0
-        for ci in range(1, len(CHUNKS)):
-            c1 = c0 + CHUNKS[ci]
-            s_t = load_scales("qs%d" % ci, queries_scales, 0, G, c0, c1)
-            c_t = load_codes("qc%d" % ci, queries_words, 0, G, c0, c1)
-            for jj in range(CHUNKS[ci] // P):
-                for g in range(G):
-                    qc[(c0 // P + jj, g)] = (c_t, g, jj)
-                    qs[(c0 // P + jj, g)] = (s_t, g, jj)
-            c0 = c1
+                qc[(c, g)] = (t, g)
+                qs[(c, g)] = (planes[c], g)
 
-        bias = keep.tile([P, C_OUT], F32, name="bias")
-        gam = keep.tile([P, H], F32, name="gam")
-        for i in range(3):
+        for c in range(1, 1 + LOAD_AHEAD):
+            load_chunk(c)
+
+        scratch = psum.tile([P, NB], F32, name="acc")
+        for i in range(WARM_BEFORE_BIAS):
+            nc.tensor.matmul(out=scratch[:], lhsT=ones[:, 0:P], rhs=ones[:], start=True, stop=True)
+        for i in range(C_OUT // NB):
             bps = psum.tile([P, NB], F32, name="acc")
-            nc.tensor.matmul(out=bps[:], lhsT=ones[:], rhs=brow[:, NB * i : NB * (i + 1)], start=True, stop=True)
-            if i < 2:
-                nc.scalar.copy(out=bias[:, NB * i : NB * (i + 1)], in_=bps[:])
-            else:
-                nc.scalar.copy(out=gam[:], in_=bps[:, 0:H])
+            nc.tensor.matmul(out=bps[:], lhsT=ones[:, 0:P], rhs=brow[:, NB * i : NB * (i + 1)], start=True, stop=True)
+            nc.scalar.copy(out=bias[:, NB * i : NB * (i + 1)], in_=bps[:])
+        for i in range(WARM_AFTER_BIAS):
+            nc.tensor.matmul(out=scratch[:], lhsT=ones[:, 0:P], rhs=ones[:], start=True, stop=True)
 
-        junk = keep.tile([P, DK], F32, name="junk")
+        units = []
+        for j in range(NTILE):
+            for c0 in range(0, C_OUT, NB):
+                units.append((j, c0, NB))
+        units = units[:-1]
+        for c0 in range(C_OUT - NB, C_OUT, TAIL_W):
+            units.append((NTILE - 1, c0, TAIL_W))
+        nunit = len(units)
 
         def mm(acc, u, g):
-            j, half = u // NHALF, u % NHALF
-            ct, gi, jj = qc[(j, g)]
-            st, gs, js = qs[(j, g)]
+            j, c0, w = units[u]
+            c, jj = j // (CHUNK // P), j % (CHUNK // P)
+            ct, gi = qc[(c, g)]
+            st, gs = qs[(c, g)]
+            wt, wi = wc[g]
             wst, wg = ws[g]
             nc.tensor.matmul_mx(
                 out=acc[:],
                 lhsT=ct[:, gi, 2 * P * jj : 2 * P * (jj + 1)].bitcast(FP4X4),
-                lhsT_scale=st[:, gs, P * js : P * (js + 1)],
-                rhs=wc[g][:, 0, 2 * NB * half : 2 * NB * (half + 1)].bitcast(FP4X4),
-                rhs_scale=wst[:, wg, NB * half : NB * (half + 1)],
+                lhsT_scale=st[:, gs, P * jj : P * (jj + 1)],
+                rhs=wt[:, wi, 2 * c0 : 2 * (c0 + w)].bitcast(FP4X4),
+                rhs_scale=wst[:, wg, c0 : c0 + w],
                 start=(g == 0),
                 stop=(g == G - 1),
             )
@@ -129,39 +162,37 @@ def tile_ufoattention_pb_kernel(tc, queries_words, queries_scales, Wq_words, Wq_
         rs = {}
 
         def add_and_square(acc, u):
-            half = u % NHALF
-            y = ypool.tile([P, NB], F32, name="y")
-            nc.vector.tensor_tensor(out=y[:], in0=acc[:], in1=bias[:, NB * half : NB * (half + 1)], op=ALU.add)
-            ss = stat.tile([P, HPU], F32, name="ss")
-            for h in range(HPU):
+            j, c0, w = units[u]
+            y = ypool.tile([P, w], F32, name="y")
+            nc.vector.tensor_tensor(out=y[:], in0=acc[:], in1=bias[:, c0 : c0 + w], op=ALU.add)
+            ss = stat.tile([P, w // DK], F32, name="ss")
+            for h in range(w // DK):
                 nc.scalar.activation(
                     out=junk[:], in_=y[:, DK * h : DK * (h + 1)], func=ACT.Square, accum_out=ss[:, h : h + 1]
                 )
-            nrm = stat.tile([P, HPU], F32, name="nrm")
-            nc.scalar.activation(out=nrm[:], in_=ss[:], func=ACT.Sqrt)
+            nrm = stat.tile([P, w // DK], F32, name="nrm")
+            nc.scalar.activation(out=nrm[:], in_=ss[:], func=ACT.Abs_reciprocal_sqrt)
             ys[u] = y
             rs[u] = nrm
 
         def scale_and_store(u):
-            j, half = u // NHALF, u % NHALF
+            j, c0, w = units[u]
             y = ys[u]
-            nrm = rs[u]
-            rinv = stat.tile([P, HPU], F32, name="rinv")
-            nc.vector.reciprocal(out=rinv[:], in_=nrm[:])
-            for h in range(HPU):
-                hh = HPU * half + h
+            nh, h0 = w // DK, c0 // DK
+            rinv = rs[u]
+            for h in range(nh):
                 nc.vector.tensor_scalar(
                     out=y[:, DK * h : DK * (h + 1)],
                     in0=y[:, DK * h : DK * (h + 1)],
                     scalar1=rinv[:, h : h + 1],
-                    scalar2=gam[:, hh : hh + 1],
+                    scalar2=gam[:, h0 + h : h0 + h + 1],
                     op0=ALU.mult,
                     op1=ALU.mult,
                 )
             b, t0 = j // (NTOK // P), (j % (NTOK // P)) * P
-            nc.scalar.dma_start(
-                out=out[b, HPU * half : HPU * (half + 1), t0 : t0 + P, :].rearrange("h t d -> t h d"),
-                in_=y[:].rearrange("p (h d) -> p h d", h=HPU),
+            nc.sync.dma_start(
+                out=out[b, h0 : h0 + nh, t0 : t0 + P, :].rearrange("h t d -> t h d"),
+                in_=y[:].rearrange("p (h d) -> p h d", h=nh),
             )
 
         accs = {}
@@ -170,12 +201,16 @@ def tile_ufoattention_pb_kernel(tc, queries_words, queries_scales, Wq_words, Wq_
         for g in range(G):
             for u in range(HEAD_UNITS):
                 mm(accs[u], u, g)
-        for u in range(NUNIT):
+        for u in range(nunit):
             if u >= HEAD_UNITS:
-                accs[u] = psum.tile([P, NB], F32, name="acc")
+                accs[u] = psum.tile([P, units[u][2]], F32, name="acc")
                 for g in range(G):
                     mm(accs[u], u, g)
             add_and_square(accs[u], u)
             if u >= 1:
                 scale_and_store(u - 1)
-        scale_and_store(NUNIT - 1)
+            if u % UNITS_PER_CHUNK == 0:
+                c = u // UNITS_PER_CHUNK + 1 + LOAD_AHEAD
+                if c < NCHUNK:
+                    load_chunk(c)
+        scale_and_store(nunit - 1)

@@ -26,9 +26,9 @@ UNITS_PER_CHUNK = (CHUNK // P) * (C_OUT // NB)
 GROUPS = ((0, 4), (4, 8))
 W_CODE_GROUPS = ((0, 1), (1, 2), (2, 3), (3, 4), (4, 6), (6, 8))
 LOAD_AHEAD = 2
-WARM_BEFORE_BIAS = 3
-WARM_AFTER_BIAS = 7
-TAIL_W = 256
+NWARM = 11
+TAIL_WIDTHS = (256, 256)
+Q0_CODE_GROUPS = ((0, 2), (2, 4), (4, 8))
 
 
 def tile_ufoattention_pb_kernel(tc, queries_words, queries_scales, Wq_words, Wq_scales, bq, gamma, out):
@@ -60,29 +60,22 @@ def tile_ufoattention_pb_kernel(tc, queries_words, queries_scales, Wq_words, Wq_
             )
             return codes
 
-        brow = keep.tile([P, C_OUT], BF16, name="brow")
         ones = keep.tile([P, NB], BF16, name="ones")
         warm = keep.tile([P, 1], F32, name="warm")
         gam_bf = keep.tile([P, H], BF16, name="gam_bf")
         gam = keep.tile([P, H], F32, name="gam")
-        bias = keep.tile([P, C_OUT], F32, name="bias")
+        bias = keep.tile([P, C_OUT], BF16, name="bias")
         junk = keep.tile([P, DK], F32, name="junk")
-        nc.gpsimd.memset(warm[:], 1.0)
-        nc.gpsimd.memset(brow[:].bitcast(F32), 0.0)
-        nc.scalar.dma_start(out=brow[0:1, :], in_=bq.rearrange("(o n) -> o n", o=1))
-        nc.gpsimd.memset(ones[:], 1.0)
-        nc.gpsimd.dma_start(out=gam_bf[:], in_=gamma.rearrange("a h b c -> (a h b c)").partition_broadcast(P))
-        nc.scalar.activation(out=warm[:], in_=warm[:], func=ACT.Abs_reciprocal_sqrt)
 
         (a0, a1), (b0, b1) = GROUPS
         wsA = new_plane("wsa", a0, a1, C_OUT)
         qsA = new_plane("qs0a", a0, a1, CHUNK)
+        nc.vector.memset(ones[:], 1.0)
         wsB = new_plane("wsb", b0, b1, C_OUT)
         qsB = new_plane("qs0b", b0, b1, CHUNK)
         planes = {}
         for c in range(1, NCHUNK):
             planes[c] = new_plane("qs%d" % c, 0, G, CHUNK)
-        nc.vector.tensor_copy(out=gam[:], in_=gam_bf[:])
 
         wc = {}
         ws = {}
@@ -95,21 +88,32 @@ def tile_ufoattention_pb_kernel(tc, queries_words, queries_scales, Wq_words, Wq_
             for g in range(g0, g1):
                 wc[g] = (t, g - g0)
 
+        def load_q0_codes(i):
+            g0, g1 = Q0_CODE_GROUPS[i]
+            t = load_codes("qc0_%d" % i, queries_words, g0, g1, 0, CHUNK)
+            for g in range(g0, g1):
+                qc[(0, g)] = (t, g - g0)
+
         load_w_codes(0)
-        qcA = load_codes("qc0a", queries_words, a0, a1, 0, CHUNK)
+        load_q0_codes(0)
+        nc.gpsimd.memset(warm[:], 1.0)
+        nc.scalar.activation(out=warm[:], in_=warm[:], func=ACT.Abs_reciprocal_sqrt)
+        nc.gpsimd.dma_start(out=gam_bf[:], in_=gamma.rearrange("a h b c -> (a h b c)").partition_broadcast(P))
+        nc.vector.tensor_copy(out=gam[:], in_=gam_bf[:])
         load_scales(wsA, Wq_scales, a0, a1, 0, C_OUT)
         load_scales(qsA, queries_scales, a0, a1, 0, CHUNK)
         load_w_codes(1)
         load_w_codes(2)
+        load_q0_codes(1)
         load_w_codes(3)
         load_scales(wsB, Wq_scales, b0, b1, 0, C_OUT)
         load_scales(qsB, queries_scales, b0, b1, 0, CHUNK)
-        qcB = load_codes("qc0b", queries_words, b0, b1, 0, CHUNK)
         load_w_codes(4)
+        load_q0_codes(2)
         load_w_codes(5)
+        nc.sync.dma_start(out=bias[:], in_=bq.partition_broadcast(P))
         for g in range(G):
             ws[g] = (wsA, g - a0) if g < a1 else (wsB, g - b0)
-            qc[(0, g)] = (qcA, g - a0) if g < a1 else (qcB, g - b0)
             qs[(0, g)] = (qsA, g - a0) if g < a1 else (qsB, g - b0)
 
         def load_chunk(c):
@@ -123,13 +127,7 @@ def tile_ufoattention_pb_kernel(tc, queries_words, queries_scales, Wq_words, Wq_
             load_chunk(c)
 
         scratch = psum.tile([P, NB], F32, name="acc")
-        for i in range(WARM_BEFORE_BIAS):
-            nc.tensor.matmul(out=scratch[:], lhsT=ones[:, 0:P], rhs=ones[:], start=True, stop=True)
-        for i in range(C_OUT // NB):
-            bps = psum.tile([P, NB], F32, name="acc")
-            nc.tensor.matmul(out=bps[:], lhsT=ones[:, 0:P], rhs=brow[:, NB * i : NB * (i + 1)], start=True, stop=True)
-            nc.scalar.copy(out=bias[:, NB * i : NB * (i + 1)], in_=bps[:])
-        for i in range(WARM_AFTER_BIAS):
+        for i in range(NWARM):
             nc.tensor.matmul(out=scratch[:], lhsT=ones[:, 0:P], rhs=ones[:], start=True, stop=True)
 
         units = []
@@ -137,8 +135,10 @@ def tile_ufoattention_pb_kernel(tc, queries_words, queries_scales, Wq_words, Wq_
             for c0 in range(0, C_OUT, NB):
                 units.append((j, c0, NB))
         units = units[:-1]
-        for c0 in range(C_OUT - NB, C_OUT, TAIL_W):
-            units.append((NTILE - 1, c0, TAIL_W))
+        c0 = C_OUT - NB
+        for w in TAIL_WIDTHS:
+            units.append((NTILE - 1, c0, w))
+            c0 += w
         nunit = len(units)
 
         def mm(acc, u, g):

@@ -23,10 +23,10 @@ HEAD_UNITS = 8
 CHUNK = 512
 NCHUNK = T // CHUNK
 UNITS_PER_CHUNK = (CHUNK // P) * (C_OUT // NB)
-GROUPS = ((0, 4), (4, 8))
+PLANE_GROUPS = ((0, 2), (2, 4), (4, 8))
 W_CODE_GROUPS = ((0, 1), (1, 2), (2, 3), (3, 4), (4, 6), (6, 8))
 LOAD_AHEAD = 2
-NWARM = 11
+NWARM = 9
 TAIL_WIDTHS = (256, 256)
 Q0_CODE_GROUPS = ((0, 2), (2, 4), (4, 8))
 
@@ -45,12 +45,15 @@ def tile_ufoattention_pb_kernel(tc, queries_words, queries_scales, Wq_words, Wq_
             nc.vector.memset(plane[:].bitcast(I32), 0)
             return plane
 
+        def load_scale_rows(plane, src, g0, g1, c0, c1, q):
+            nc.sync.dma_start(
+                out=plane[32 * q : 32 * q + 4, :, :].bitcast(I32),
+                in_=src[g0:g1, 4 * q : 4 * q + 4, c0:c1].rearrange("g r n -> r g n").bitcast(I32),
+            )
+
         def load_scales(plane, src, g0, g1, c0, c1):
-            for q in range(4):
-                nc.sync.dma_start(
-                    out=plane[32 * q : 32 * q + 4, :, :].bitcast(I32),
-                    in_=src[g0:g1, 4 * q : 4 * q + 4, c0:c1].rearrange("g r n -> r g n").bitcast(I32),
-                )
+            for q in (0, 2, 1, 3):
+                load_scale_rows(plane, src, g0, g1, c0, c1, q)
 
         def load_codes(name, src, g0, g1, c0, c1):
             codes = keep.tile([P, g1 - g0, 2 * (c1 - c0)], U8, name=name, align_bytes=64)
@@ -67,12 +70,15 @@ def tile_ufoattention_pb_kernel(tc, queries_words, queries_scales, Wq_words, Wq_
         bias = keep.tile([P, C_OUT], BF16, name="bias")
         junk = keep.tile([P, DK], F32, name="junk")
 
-        (a0, a1), (b0, b1) = GROUPS
-        wsA = new_plane("wsa", a0, a1, C_OUT)
-        qsA = new_plane("qs0a", a0, a1, CHUNK)
+        (a0, a1) = PLANE_GROUPS[0]
+        q0_planes = [keep.tile([P, a1 - a0, CHUNK], U8, name="qs0_0", align_bytes=64)]
+        nc.gpsimd.memset(q0_planes[0][:].bitcast(F32), 0.0)
+        w_planes = [new_plane("ws0", a0, a1, C_OUT)]
         nc.vector.memset(ones[:], 1.0)
-        wsB = new_plane("wsb", b0, b1, C_OUT)
-        qsB = new_plane("qs0b", b0, b1, CHUNK)
+        for i in range(1, len(PLANE_GROUPS)):
+            g0, g1 = PLANE_GROUPS[i]
+            q0_planes.append(new_plane("qs0_%d" % i, g0, g1, CHUNK))
+            w_planes.append(new_plane("ws%d" % i, g0, g1, C_OUT))
         planes = {}
         for c in range(1, NCHUNK):
             planes[c] = new_plane("qs%d" % c, 0, G, CHUNK)
@@ -94,27 +100,42 @@ def tile_ufoattention_pb_kernel(tc, queries_words, queries_scales, Wq_words, Wq_
             for g in range(g0, g1):
                 qc[(0, g)] = (t, g - g0)
 
-        load_w_codes(0)
+        def load_q0_scales(i):
+            g0, g1 = PLANE_GROUPS[i]
+            load_scales(q0_planes[i], queries_scales, g0, g1, 0, CHUNK)
+
+        def load_w_scales(i):
+            g0, g1 = PLANE_GROUPS[i]
+            load_scales(w_planes[i], Wq_scales, g0, g1, 0, C_OUT)
+
+        load_scale_rows(q0_planes[0], queries_scales, a0, a1, 0, CHUNK, 0)
+        load_scale_rows(q0_planes[0], queries_scales, a0, a1, 0, CHUNK, 2)
         load_q0_codes(0)
+        load_w_codes(0)
+        load_scale_rows(q0_planes[0], queries_scales, a0, a1, 0, CHUNK, 1)
+        load_scale_rows(q0_planes[0], queries_scales, a0, a1, 0, CHUNK, 3)
+        load_w_scales(0)
         nc.gpsimd.memset(warm[:], 1.0)
         nc.scalar.activation(out=warm[:], in_=warm[:], func=ACT.Abs_reciprocal_sqrt)
         nc.gpsimd.dma_start(out=gam_bf[:], in_=gamma.rearrange("a h b c -> (a h b c)").partition_broadcast(P))
         nc.vector.tensor_copy(out=gam[:], in_=gam_bf[:])
-        load_scales(wsA, Wq_scales, a0, a1, 0, C_OUT)
-        load_scales(qsA, queries_scales, a0, a1, 0, CHUNK)
         load_w_codes(1)
         load_w_codes(2)
         load_q0_codes(1)
+        load_q0_scales(1)
+        load_w_scales(1)
         load_w_codes(3)
-        load_scales(wsB, Wq_scales, b0, b1, 0, C_OUT)
-        load_scales(qsB, queries_scales, b0, b1, 0, CHUNK)
+        load_q0_scales(2)
+        load_w_scales(2)
         load_w_codes(4)
         load_q0_codes(2)
         load_w_codes(5)
         nc.sync.dma_start(out=bias[:], in_=bq.partition_broadcast(P))
-        for g in range(G):
-            ws[g] = (wsA, g - a0) if g < a1 else (wsB, g - b0)
-            qs[(0, g)] = (qsA, g - a0) if g < a1 else (qsB, g - b0)
+        for i in range(len(PLANE_GROUPS)):
+            g0, g1 = PLANE_GROUPS[i]
+            for g in range(g0, g1):
+                ws[g] = (w_planes[i], g - g0)
+                qs[(0, g)] = (q0_planes[i], g - g0)
 
         def load_chunk(c):
             load_scales(planes[c], queries_scales, 0, G, CHUNK * c, CHUNK * (c + 1))

@@ -71,8 +71,7 @@ def tile_ufoattention_pb_kernel(tc, queries_words, queries_scales, Wq_words, Wq_
         junk = keep.tile([P, DK], F32, name="junk")
 
         (a0, a1) = PLANE_GROUPS[0]
-        q0_planes = [keep.tile([P, a1 - a0, CHUNK], U8, name="qs0_0", align_bytes=64)]
-        nc.gpsimd.memset(q0_planes[0][:].bitcast(F32), 0.0)
+        q0_planes = [new_plane("qs0_0", a0, a1, CHUNK)]
         w_planes = [new_plane("ws0", a0, a1, C_OUT)]
         nc.vector.memset(ones[:], 1.0)
         for i in range(1, len(PLANE_GROUPS)):

@@ -23,8 +23,9 @@ HEAD_UNITS = 8
 CHUNK = 512
 NCHUNK = T // CHUNK
 UNITS_PER_CHUNK = (CHUNK // P) * (C_OUT // NB)
-PLANE_GROUPS = ((0, 2), (2, 4), (4, 8))
-W_CODE_GROUPS = ((0, 1), (1, 2), (2, 3), (3, 4), (4, 6), (6, 8))
+W_PLANE_GROUPS = ((0, 2), (2, 5), (5, 8))
+Q0_PLANE_GROUPS = ((0, 4), (4, 8))
+W_CODE_GROUPS = ((0, 1), (1, 2), (2, 4), (4, 6), (6, 8))
 LOAD_AHEAD = 2
 NWARM = 9
 TAIL_WIDTHS = (256, 256)
@@ -70,14 +71,12 @@ def tile_ufoattention_pb_kernel(tc, queries_words, queries_scales, Wq_words, Wq_
         bias = keep.tile([P, C_OUT], BF16, name="bias")
         junk = keep.tile([P, DK], F32, name="junk")
 
-        (a0, a1) = PLANE_GROUPS[0]
-        q0_planes = [new_plane("qs0_0", a0, a1, CHUNK)]
-        w_planes = [new_plane("ws0", a0, a1, C_OUT)]
+        q0_planes = [new_plane("qs0_0", Q0_PLANE_GROUPS[0][0], Q0_PLANE_GROUPS[0][1], CHUNK)]
+        w_planes = [new_plane("ws0", W_PLANE_GROUPS[0][0], W_PLANE_GROUPS[0][1], C_OUT)]
         nc.vector.memset(ones[:], 1.0)
-        for i in range(1, len(PLANE_GROUPS)):
-            g0, g1 = PLANE_GROUPS[i]
-            q0_planes.append(new_plane("qs0_%d" % i, g0, g1, CHUNK))
-            w_planes.append(new_plane("ws%d" % i, g0, g1, C_OUT))
+        w_planes.append(new_plane("ws1", W_PLANE_GROUPS[1][0], W_PLANE_GROUPS[1][1], C_OUT))
+        q0_planes.append(new_plane("qs0_1", Q0_PLANE_GROUPS[1][0], Q0_PLANE_GROUPS[1][1], CHUNK))
+        w_planes.append(new_plane("ws2", W_PLANE_GROUPS[2][0], W_PLANE_GROUPS[2][1], C_OUT))
         planes = {}
         for c in range(1, NCHUNK):
             planes[c] = new_plane("qs%d" % c, 0, G, CHUNK)
@@ -99,20 +98,19 @@ def tile_ufoattention_pb_kernel(tc, queries_words, queries_scales, Wq_words, Wq_
             for g in range(g0, g1):
                 qc[(0, g)] = (t, g - g0)
 
-        def load_q0_scales(i):
-            g0, g1 = PLANE_GROUPS[i]
-            load_scales(q0_planes[i], queries_scales, g0, g1, 0, CHUNK)
+        def load_q0_scales(i, quadrants):
+            g0, g1 = Q0_PLANE_GROUPS[i]
+            for q in quadrants:
+                load_scale_rows(q0_planes[i], queries_scales, g0, g1, 0, CHUNK, q)
 
         def load_w_scales(i):
-            g0, g1 = PLANE_GROUPS[i]
+            g0, g1 = W_PLANE_GROUPS[i]
             load_scales(w_planes[i], Wq_scales, g0, g1, 0, C_OUT)
 
-        load_scale_rows(q0_planes[0], queries_scales, a0, a1, 0, CHUNK, 0)
-        load_scale_rows(q0_planes[0], queries_scales, a0, a1, 0, CHUNK, 2)
+        load_q0_scales(0, (0, 2))
         load_q0_codes(0)
         load_w_codes(0)
-        load_scale_rows(q0_planes[0], queries_scales, a0, a1, 0, CHUNK, 1)
-        load_scale_rows(q0_planes[0], queries_scales, a0, a1, 0, CHUNK, 3)
+        load_q0_scales(0, (1, 3))
         load_w_scales(0)
         nc.gpsimd.memset(warm[:], 1.0)
         nc.scalar.activation(out=warm[:], in_=warm[:], func=ACT.Abs_reciprocal_sqrt)
@@ -121,19 +119,20 @@ def tile_ufoattention_pb_kernel(tc, queries_words, queries_scales, Wq_words, Wq_
         load_w_codes(1)
         load_w_codes(2)
         load_q0_codes(1)
-        load_q0_scales(1)
         load_w_scales(1)
+        load_q0_scales(1, (0, 2, 1, 3))
         load_w_codes(3)
-        load_q0_scales(2)
+        load_q0_codes(2)
         load_w_scales(2)
         load_w_codes(4)
-        load_q0_codes(2)
-        load_w_codes(5)
         nc.sync.dma_start(out=bias[:], in_=bq.partition_broadcast(P))
-        for i in range(len(PLANE_GROUPS)):
-            g0, g1 = PLANE_GROUPS[i]
+        for i in range(len(W_PLANE_GROUPS)):
+            g0, g1 = W_PLANE_GROUPS[i]
             for g in range(g0, g1):
                 ws[g] = (w_planes[i], g - g0)
+        for i in range(len(Q0_PLANE_GROUPS)):
+            g0, g1 = Q0_PLANE_GROUPS[i]
+            for g in range(g0, g1):
                 qs[(0, g)] = (q0_planes[i], g - g0)
 
         def load_chunk(c):

@@ -28,7 +28,7 @@ Q0_PLANE_GROUPS = ((0, 4), (4, 8))
 W_CODE_GROUPS = ((0, 1), (1, 2), (2, 4), (4, 6), (6, 8))
 LOAD_AHEAD = 2
 NWARM = 9
-TAIL_WIDTHS = (256, 256)
+TAIL_WIDTHS = (256, 128, 128)
 Q0_CODE_GROUPS = ((0, 2), (2, 4), (4, 8))
 
 

@@ -27,7 +27,7 @@ W_PLANE_GROUPS = ((0, 2), (2, 5), (5, 8))
 Q0_PLANE_GROUPS = ((0, 4), (4, 8))
 W_CODE_GROUPS = ((0, 1), (1, 2), (2, 4), (4, 6), (6, 8))
 LOAD_AHEAD = 2
-NWARM = 9
+NWARM = 7
 TAIL_WIDTHS = (256, 128, 128)
 Q0_CODE_GROUPS = ((0, 2), (2, 4), (4, 8))
 
@@ -46,10 +46,10 @@ def tile_ufoattention_pb_kernel(tc, queries_words, queries_scales, Wq_words, Wq_
             nc.vector.memset(plane[:].bitcast(I32), 0)
             return plane
 
-        def load_scale_rows(plane, src, g0, g1, c0, c1, q):
+        def load_scale_rows(plane, src, g0, g1, c0, c1, r):
             nc.sync.dma_start(
-                out=plane[32 * q : 32 * q + 4, :, :].bitcast(I32),
-                in_=src[g0:g1, 4 * q : 4 * q + 4, c0:c1].rearrange("g r n -> r g n").bitcast(I32),
+                out=plane[r : P : 32, :, :].bitcast(I32),
+                in_=src[g0:g1, r : 16 : 4, c0:c1].rearrange("g q n -> q g n").bitcast(I32),
             )
 
         def load_scales(plane, src, g0, g1, c0, c1):

@@ -27,7 +27,7 @@ W_PLANE_GROUPS = ((0, 2), (2, 5), (5, 8))
 Q0_PLANE_GROUPS = ((0, 4), (4, 8))
 W_CODE_GROUPS = ((0, 1), (1, 2), (2, 4), (4, 6), (6, 8))
 LOAD_AHEAD = 2
-NWARM = 7
+NWARM = 9
 TAIL_WIDTHS = (256, 128, 128)
 Q0_CODE_GROUPS = ((0, 2), (2, 4), (4, 8))
 
@@ -42,7 +42,7 @@ def tile_ufoattention_pb_kernel(tc, queries_words, queries_scales, Wq_words, Wq_
         ctx.enter_context(tc.manual_schedule())
 
         def new_plane(name, g0, g1, width):
-            plane = keep.tile([P, g1 - g0, width], U8, name=name, align_bytes=64)
+            plane = keep.tile([P, g1 - g0, width], U8, name=name, align_bytes=256)
             nc.vector.memset(plane[:].bitcast(I32), 0)
             return plane
 
@@ -57,7 +57,7 @@ def tile_ufoattention_pb_kernel(tc, queries_words, queries_scales, Wq_words, Wq_
                 load_scale_rows(plane, src, g0, g1, c0, c1, q)
 
         def load_codes(name, src, g0, g1, c0, c1):
-            codes = keep.tile([P, g1 - g0, 2 * (c1 - c0)], U8, name=name, align_bytes=64)
+            codes = keep.tile([P, g1 - g0, 2 * (c1 - c0)], U8, name=name, align_bytes=256)
             nc.sync.dma_start(
                 out=codes[:].bitcast(I32),
                 in_=src[g0:g1, :, 2 * c0 : 2 * c1].rearrange("g p n -> p g n").bitcast(I32),

from contextlib import ExitStack

import concourse.mybir as mybir

F32 = mybir.dt.float32
BF16 = mybir.dt.bfloat16
U8 = mybir.dt.uint8
I32 = mybir.dt.int32
FP4X4 = mybir.dt.float4_e2m1fn_x4
ACT = mybir.ActivationFunctionType
ALU = mybir.AluOpType

B, NTOK, D, H, DK = 4, 1536, 4096, 8, 128
T = B * NTOK
C_OUT = H * DK
FLOPS = 2 * T * D * C_OUT

P = 128
G = D // 512
NB = 512
NTILE = T // P
HEAD_UNITS = 8
CHUNK = 512
NCHUNK = T // CHUNK
UNITS_PER_CHUNK = (CHUNK // P) * (C_OUT // NB)
W_PLANE_GROUPS = ((0, 2), (2, 5), (5, 8))
Q0_PLANE_GROUPS = ((0, 4), (4, 8))
W_CODE_GROUPS = ((0, 1), (1, 2), (2, 4), (4, 6), (6, 8))
LOAD_AHEAD = 2
NWARM = 9
TAIL_WIDTHS = (256, 128, 128)
Q0_CODE_GROUPS = ((0, 2), (2, 4), (4, 8))


def tile_ufoattention_pb_kernel(tc, queries_words, queries_scales, Wq_words, Wq_scales, bq, gamma, out):
    nc = tc.nc
    with ExitStack() as ctx:
        keep = ctx.enter_context(tc.tile_pool(name="keep", bufs=1))
        ypool = ctx.enter_context(tc.tile_pool(name="ypool", bufs=8))
        stat = ctx.enter_context(tc.tile_pool(name="stat", bufs=4))
        psum = ctx.enter_context(tc.psum_pool(name="psum", bufs=8))
        ctx.enter_context(tc.manual_schedule())

        def new_plane(name, g0, g1, width):
            plane = keep.tile([P, g1 - g0, width], U8, name=name, align_bytes=256)
            nc.vector.memset(plane[:].bitcast(I32), 0)
            return plane

        def load_scale_rows(plane, src, g0, g1, c0, c1, r):
            nc.sync.dma_start(
                out=plane[r : P : 32, :, :].bitcast(I32),
                in_=src[g0:g1, r : 16 : 4, c0:c1].rearrange("g q n -> q g n").bitcast(I32),
            )

        def load_scales(plane, src, g0, g1, c0, c1):
            for q in (0, 2, 1, 3):
                load_scale_rows(plane, src, g0, g1, c0, c1, q)

        def load_codes(name, src, g0, g1, c0, c1):
            codes = keep.tile([P, g1 - g0, 2 * (c1 - c0)], U8, name=name, align_bytes=256)
            nc.sync.dma_start(
                out=codes[:].bitcast(I32),
                in_=src[g0:g1, :, 2 * c0 : 2 * c1].rearrange("g p n -> p g n").bitcast(I32),
            )
            return codes

        ones = keep.tile([P, NB], BF16, name="ones")
        warm = keep.tile([P, 1], F32, name="warm")
        gam_bf = keep.tile([P, H], BF16, name="gam_bf")
        gam = keep.tile([P, H], F32, name="gam")
        bias = keep.tile([P, C_OUT], BF16, name="bias")
        junk = keep.tile([P, DK], F32, name="junk")

        q0_planes = [new_plane("qs0_0", Q0_PLANE_GROUPS[0][0], Q0_PLANE_GROUPS[0][1], CHUNK)]
        w_planes = [new_plane("ws0", W_PLANE_GROUPS[0][0], W_PLANE_GROUPS[0][1], C_OUT)]
        nc.vector.memset(ones[:], 1.0)
        w_planes.append(new_plane("ws1", W_PLANE_GROUPS[1][0], W_PLANE_GROUPS[1][1], C_OUT))
        q0_planes.append(new_plane("qs0_1", Q0_PLANE_GROUPS[1][0], Q0_PLANE_GROUPS[1][1], CHUNK))
        w_planes.append(new_plane("ws2", W_PLANE_GROUPS[2][0], W_PLANE_GROUPS[2][1], C_OUT))
        planes = {}
        for c in range(1, NCHUNK):
            planes[c] = new_plane("qs%d" % c, 0, G, CHUNK)

        wc = {}
        ws = {}
        qc = {}
        qs = {}

        def load_w_codes(i):
            g0, g1 = W_CODE_GROUPS[i]
            t = load_codes("wc%d" % i, Wq_words, g0, g1, 0, C_OUT)
            for g in range(g0, g1):
                wc[g] = (t, g - g0)

        def load_q0_codes(i):
            g0, g1 = Q0_CODE_GROUPS[i]
            t = load_codes("qc0_%d" % i, queries_words, g0, g1, 0, CHUNK)
            for g in range(g0, g1):
                qc[(0, g)] = (t, g - g0)

        def load_q0_scales(i, quadrants):
            g0, g1 = Q0_PLANE_GROUPS[i]
            for q in quadrants:
                load_scale_rows(q0_planes[i], queries_scales, g0, g1, 0, CHUNK, q)

        def load_w_scales(i):
            g0, g1 = W_PLANE_GROUPS[i]
            load_scales(w_planes[i], Wq_scales, g0, g1, 0, C_OUT)

        load_q0_scales(0, (0, 2))
        load_q0_codes(0)
        load_w_codes(0)
        load_q0_scales(0, (1, 3))
        load_w_scales(0)
        nc.gpsimd.memset(warm[:], 1.0)
        nc.scalar.activation(out=warm[:], in_=warm[:], func=ACT.Abs_reciprocal_sqrt)
        nc.gpsimd.dma_start(out=gam_bf[:], in_=gamma.rearrange("a h b c -> (a h b c)").partition_broadcast(P))
        nc.vector.tensor_copy(out=gam[:], in_=gam_bf[:])
        load_w_codes(1)
        load_w_codes(2)
        load_q0_codes(1)
        load_w_scales(1)
        load_q0_scales(1, (0, 2, 1, 3))
        load_w_codes(3)
        load_q0_codes(2)
        load_w_scales(2)
        load_w_codes(4)
        nc.sync.dma_start(out=bias[:], in_=bq.partition_broadcast(P))
        for i in range(len(W_PLANE_GROUPS)):
            g0, g1 = W_PLANE_GROUPS[i]
            for g in range(g0, g1):
                ws[g] = (w_planes[i], g - g0)
        for i in range(len(Q0_PLANE_GROUPS)):
            g0, g1 = Q0_PLANE_GROUPS[i]
            for g in range(g0, g1):
                qs[(0, g)] = (q0_planes[i], g - g0)

        def load_chunk(c):
            load_scales(planes[c], queries_scales, 0, G, CHUNK * c, CHUNK * (c + 1))
            t = load_codes("qc%d" % c, queries_words, 0, G, CHUNK * c, CHUNK * (c + 1))
            for g in range(G):
                qc[(c, g)] = (t, g)
                qs[(c, g)] = (planes[c], g)

        for c in range(1, 1 + LOAD_AHEAD):
            load_chunk(c)

        scratch = psum.tile([P, NB], F32, name="acc")
        for i in range(NWARM):
            nc.tensor.matmul(out=scratch[:], lhsT=ones[:, 0:P], rhs=ones[:], start=True, stop=True)

        units = []
        for j in range(NTILE):
            for c0 in range(0, C_OUT, NB):
                units.append((j, c0, NB))
        units = units[:-1]
        c0 = C_OUT - NB
        for w in TAIL_WIDTHS:
            units.append((NTILE - 1, c0, w))
            c0 += w
        nunit = len(units)

        def mm(acc, u, g):
            j, c0, w = units[u]
            c, jj = j // (CHUNK // P), j % (CHUNK // P)
            ct, gi = qc[(c, g)]
            st, gs = qs[(c, g)]
            wt, wi = wc[g]
            wst, wg = ws[g]
            nc.tensor.matmul_mx(
                out=acc[:],
                lhsT=ct[:, gi, 2 * P * jj : 2 * P * (jj + 1)].bitcast(FP4X4),
                lhsT_scale=st[:, gs, P * jj : P * (jj + 1)],
                rhs=wt[:, wi, 2 * c0 : 2 * (c0 + w)].bitcast(FP4X4),
                rhs_scale=wst[:, wg, c0 : c0 + w],
                start=(g == 0),
                stop=(g == G - 1),
            )

        ys = {}
        rs = {}

        def add_and_square(acc, u):
            j, c0, w = units[u]
            y = ypool.tile([P, w], F32, name="y")
            nc.vector.tensor_tensor(out=y[:], in0=acc[:], in1=bias[:, c0 : c0 + w], op=ALU.add)
            ss = stat.tile([P, w // DK], F32, name="ss")
            for h in range(w // DK):
                nc.scalar.activation(
                    out=junk[:], in_=y[:, DK * h : DK * (h + 1)], func=ACT.Square, accum_out=ss[:, h : h + 1]
                )
            nrm = stat.tile([P, w // DK], F32, name="nrm")
            nc.scalar.activation(out=nrm[:], in_=ss[:], func=ACT.Abs_reciprocal_sqrt)
            ys[u] = y
            rs[u] = nrm

        def scale_and_store(u):
            j, c0, w = units[u]
            y = ys[u]
            nh, h0 = w // DK, c0 // DK
            rinv = rs[u]
            for h in range(nh):
                nc.vector.tensor_scalar(
                    out=y[:, DK * h : DK * (h + 1)],
                    in0=y[:, DK * h : DK * (h + 1)],
                    scalar1=rinv[:, h : h + 1],
                    scalar2=gam[:, h0 + h : h0 + h + 1],
                    op0=ALU.mult,
                    op1=ALU.mult,
                )
            b, t0 = j // (NTOK // P), (j % (NTOK // P)) * P
            nc.sync.dma_start(
                out=out[b, h0 : h0 + nh, t0 : t0 + P, :].rearrange("h t d -> t h d"),
                in_=y[:].rearrange("p (h d) -> p h d", h=nh),
            )

        accs = {}
        for u in range(HEAD_UNITS):
            accs[u] = psum.tile([P, NB], F32, name="acc")
        for g in range(G):
            for u in range(HEAD_UNITS):
                mm(accs[u], u, g)
        for u in range(nunit):
            if u >= HEAD_UNITS:
                accs[u] = psum.tile([P, units[u][2]], F32, name="acc")
                for g in range(G):
                    mm(accs[u], u, g)
            add_and_square(accs[u], u)
            if u >= 1:
                scale_and_store(u - 1)
            if u % UNITS_PER_CHUNK == 0:
                c = u // UNITS_PER_CHUNK + 1 + LOAD_AHEAD
                if c < NCHUNK:
                    load_chunk(c)
        scale_and_store(nunit - 1)
